import numpy as np
import ml_dtypes


def mxq(x, axis, fmt="e4m3"):
    dtype, down = {"e4m3": (ml_dtypes.float8_e4m3fn, 7), "e5m2": (ml_dtypes.float8_e5m2, 14)}[fmt]
    v = np.moveaxis(np.asarray(x, np.float32).astype(ml_dtypes.bfloat16).astype(np.float64), axis, -1)
    blocks = v.reshape(v.shape[:-1] + (-1, 32))
    amax = np.abs(blocks).max(-1, keepdims=True)
    byte = np.maximum(np.where(amax > 0, np.frexp(amax)[1] - 1 + 127, 0) - down, 1)
    scale = np.exp2(byte - 127.0)
    codes = (blocks / scale).astype(np.float32).astype(dtype).astype(np.float64)
    return np.moveaxis((codes * scale).reshape(v.shape), -1, axis)


WIDE = False


def mx_kscale(k):
    if not WIDE:
        return np.ones(k)
    levels = np.array([10, -10, 5, -5, 0])
    if k % 512:
        return np.exp2(np.random.permutation(np.resize(levels, k // 32))).repeat(32)
    a = np.empty((k // 512, 16))
    for p in range(k // 512):
        a[p, :8] = np.random.permutation(np.resize(levels, 8))
        for g in range(8):
            far = levels[np.abs(levels - a[p, g]) >= 10]
            a[p, g + 8] = far[np.random.randint(len(far))]
    return np.exp2(a.ravel()).repeat(32)


BF16 = ml_dtypes.bfloat16


def bf(x):
    return np.asarray(x, np.float32).astype(BF16)


def f64(x):
    return np.asarray(x).astype(np.float64)


B, L, D, E, W1, C, F_LEN = 8, 1024, 511, 512, 8, 128, 4
SR = 0.55
WS = 0.7
KEEP = 0.75


def setup_inputs():
    s = mx_kscale(E)
    st = np.random.standard_normal((B, L, E)) * SR
    st[..., 0] = 1.0
    return {"state": bf(st * s),
            "Wg": bf(np.random.standard_normal((C, W1, E)) * WS / np.sqrt(E) / s),
            "Mg": bf(np.random.random((C, W1, E)) < KEEP),
            "bg": bf(1.0 + 0.1 * np.random.standard_normal((C, W1)))}


def reference(state, Wg, Mg, bg):
    wm = f64(Wg) * f64(Mg)
    sq = mxq(f64(state).reshape(B * L, E), 1, "e4m3")
    wq = mxq(wm.reshape(C * W1, E), 1, "e4m3")
    h = (sq @ wq.T).reshape(B, L, C, W1) + f64(bg)
    return np.prod(h, axis=-1)

@@ -1,0 +1,245 @@
+from contextlib import ExitStack
+
+import concourse.mybir as mybir
+from concourse.masks import make_identity
+
+FP8X4 = mybir.dt.float8_e4m3fn_x4
+BF16 = mybir.dt.bfloat16
+F32 = mybir.dt.float32
+U32 = mybir.dt.uint32
+U8 = mybir.dt.uint8
+ADD = mybir.AluOpType.add
+MULT = mybir.AluOpType.mult
+IDENTITY = mybir.ActivationFunctionType.Identity
+
+P = 128
+E = 512
+WORDS = E // 2
+TOKENS = 8 * 1024
+FORMS = 8
+ROUND = 512
+ROUNDS = TOKENS // ROUND
+ROUND_BLOCKS = ROUND // P
+PAIR = 2
+PAIR_ROWS = PAIR * P
+WEIGHT_PAIRS = FORMS // PAIR
+BANKS = 8
+AHEAD = 3
+BEHIND = 2
+PARTIALS = 9
+
+CHAIN_A = (0, 1, 2, 3)
+CHAIN_B = (4, 5)
+CHAIN_C = (6, 7)
+
+FLOPS = 2 * TOKENS * P * FORMS * E
+
+
+def tile_ac_filter_prenorm_net_nd_pa_t_kernel(tc, state, Wg, Mg, bg, out):
+    nc = tc.nc
+
+    state_rounds = state.flatten_outer_dims().rearrange("(r p a) e -> r p (a e)", p=P, a=ROUND_BLOCKS)
+    out_rounds = out.flatten_outer_dims().rearrange("(r p a) c -> r p (a c)", p=P, a=ROUND_BLOCKS)
+    wg_rows = Wg.rearrange("c j e -> c (j e)")
+    mg_rows = Mg.rearrange("c j e -> c (j e)")
+
+    with ExitStack() as ctx:
+        keep = ctx.enter_context(tc.tile_pool(name="keep", bufs=1))
+        stage = ctx.enter_context(tc.tile_pool(name="stage", bufs=2))
+        psum = ctx.enter_context(tc.psum_pool(name="psum", bufs=BANKS))
+        ctx.enter_context(tc.manual_schedule())
+
+        bg_sb = keep.tile([P, FORMS], BF16)
+        nc.scalar.dma_start(out=bg_sb[:], in_=bg)
+        state_sb = []
+        wg_sb = []
+        mg_sb = []
+
+        def load_state(r):
+            state_round = keep.tile([P, ROUND_BLOCKS * E], BF16, name="state_%d" % r)
+            nc.sync.dma_start(out=state_round[:], in_=state_rounds[r])
+            state_sb.append(state_round)
+
+        load_state(0)
+        for pair in range(WEIGHT_PAIRS):
+            cols = slice(pair * PAIR * E, (pair + 1) * PAIR * E)
+            wg_pair = keep.tile([P, PAIR * E], BF16, name="wg_%d" % pair)
+            mg_pair = keep.tile([P, PAIR * E], BF16, name="mg_%d" % pair)
+            nc.sync.dma_start(out=wg_pair[:], in_=wg_rows[:, cols])
+            nc.sync.dma_start(out=mg_pair[:], in_=mg_rows[:, cols])
+            wg_sb.append(wg_pair)
+            mg_sb.append(mg_pair)
+        for r in range(1, ROUNDS):
+            load_state(r)
+
+        identity = keep.tile([P, P], F32)
+        make_identity(nc, identity[:])
+        bias = keep.tile([P, FORMS], F32)
+        nc.scalar.activation(out=bias[:], in_=bg_sb[:], func=IDENTITY)
+
+        def next_bank():
+            bank = psum.tile([P, ROUND], F32, tag="bank")
+            return bank
+
+        def transpose_pair(words):
+            flipped = next_bank()
+            for b in range(PAIR):
+                for u in range(2):
+                    nc.tensor.transpose(
+                        flipped[:, u * PAIR_ROWS + b * P : u * PAIR_ROWS + (b + 1) * P],
+                        words[:, b * WORDS + u : (b + 1) * WORDS : 2],
+                        identity[:],
+                    )
+            return flipped
+
+        def regroup_pair(flipped, grouped):
+            nc.scalar.copy(
+                out=grouped.bitcast(F32).rearrange("p (n u) -> p n u", u=2),
+                in_=flipped[:].rearrange("p (u n) -> p n u", u=2),
+            )
+
+        flipped_state = {}
+        grouped_state = {}
+        quantised = {}
+        chains = {}
+        results = {}
+        backs = {}
+
+        def is_round(r):
+            return 0 <= r < ROUNDS
+
+        def transpose_state(r):
+            if is_round(r):
+                words = state_sb[r][:].bitcast(F32)
+                half_words = PAIR * WORDS
+                flipped_state[r] = [transpose_pair(words[:, h * half_words : (h + 1) * half_words]) for h in range(2)]
+
+        def regroup_state(r):
+            if is_round(r):
+                grouped = stage.tile([P, ROUND * 4], BF16, align_bytes=64)
+                half_cols = PAIR_ROWS * 4
+                for h in range(2):
+                    regroup_pair(flipped_state[r][h], grouped[:, h * half_cols : (h + 1) * half_cols])
+                grouped_state[r] = grouped
+
+        def quantise_state(r):
+            if is_round(r):
+                codes = stage.tile([P, ROUND], U32, align_bytes=64, tag="x_codes", bufs=AHEAD + 1)
+                scales = stage.tile([P, ROUND], U8, align_bytes=64, tag="x_scales", bufs=AHEAD + 1)
+                nc.vector.quantize_mx(out=codes[:].bitcast(FP8X4), scales=scales[:], in_=grouped_state[r][:])
+                quantised[r] = (codes, scales)
+
+        def form(r, j):
+            bank = next_bank()
+            codes, scales = quantised[r]
+            cols = slice(j * P, (j + 1) * P)
+            nc.tensor.matmul_mx(
+                out=bank[:],
+                lhsT=w_codes[:, cols].bitcast(FP8X4),
+                lhsT_scale=w_scales[:, cols],
+                rhs=codes[:].bitcast(FP8X4),
+                rhs_scale=scales[:],
+                start=True,
+                stop=True,
+            )
+            return bank
+
+        def partial():
+            product = stage.tile([P, ROUND], F32, tag="partial", bufs=3 * PARTIALS)
+            return product
+
+        def begin(r, chain):
+            if is_round(r):
+                j = chain[0]
+                bank = form(r, j)
+                chains[(r, chain)] = partial()
+                nc.scalar.activation(
+                    out=chains[(r, chain)][:], in_=bank[:], func=IDENTITY, bias=bias[:, j : j + 1], scale=1.0
+                )
+
+        def extend(r, chain, i):
+            if is_round(r):
+                j = chain[i]
+                bank = form(r, j)
+                longer = partial()
+                nc.vector.scalar_tensor_tensor(
+                    out=longer[:], in0=bank[:], scalar=bias[:, j : j + 1], in1=chains[(r, chain)][:], op0=ADD, op1=MULT
+                )
+                chains[(r, chain)] = longer
+
+        def join_short_chains(r):
+            if is_round(r):
+                joined = partial()
+                nc.gpsimd.tensor_tensor(
+                    out=joined[:], in0=chains[(r, CHAIN_B)][:], in1=chains[(r, CHAIN_C)][:], op=MULT
+                )
+                chains[(r, CHAIN_B)] = joined
+
+        def join_all(r):
+            if is_round(r):
+                result = stage.tile([P, ROUND], F32, bufs=BEHIND + 2)
+                nc.gpsimd.tensor_tensor(
+                    out=result[:], in0=chains[(r, CHAIN_B)][:], in1=chains[(r, CHAIN_A)][:], op=MULT
+                )
+                results[r] = result
+
+        def transpose_result(r):
+            if is_round(r):
+                backs[r] = next_bank()
+                for a in range(ROUND_BLOCKS):
+                    cols = slice(a * P, (a + 1) * P)
+                    nc.tensor.transpose(backs[r][:, cols], results[r][:, cols], identity[:])
+
+        def store_result(r):
+            if is_round(r):
+                out_sb = stage.tile([P, ROUND], F32, bufs=3)
+                nc.scalar.copy(out=out_sb[:], in_=backs[r][:])
+                nc.sync.dma_start(out=out_rounds[r], in_=out_sb[:])
+
+        w_codes = keep.tile([P, FORMS * P], U32, align_bytes=64)
+        w_scales = keep.tile([P, FORMS * P], U8, align_bytes=64)
+        w_grouped = []
+        quantise_lag = 2
+
+        def quantise_weights(pair):
+            cols = slice(pair * PAIR_ROWS, (pair + 1) * PAIR_ROWS)
+            nc.vector.quantize_mx(
+                out=w_codes[:, cols].bitcast(FP8X4), scales=w_scales[:, cols], in_=w_grouped[pair][:]
+            )
+
+        transpose_state(0)
+        regroup_state(0)
+        for pair in range(WEIGHT_PAIRS):
+            masked = keep.tile([P, PAIR * E], BF16, name="masked_%d" % pair)
+            nc.vector.tensor_tensor(out=masked[:], in0=wg_sb[pair][:], in1=mg_sb[pair][:], op=MULT)
+            if pair == 0:
+                quantise_state(0)
+            grouped = keep.tile([P, PAIR_ROWS * 4], BF16, align_bytes=64, name="w_grouped_%d" % pair)
+            regroup_pair(transpose_pair(masked[:].bitcast(F32)), grouped[:])
+            w_grouped.append(grouped)
+            if pair >= quantise_lag:
+                quantise_weights(pair - quantise_lag)
+        for pair in range(WEIGHT_PAIRS - quantise_lag, WEIGHT_PAIRS):
+            quantise_weights(pair)
+        for r in range(1, AHEAD - 1):
+            transpose_state(r)
+            regroup_state(r)
+            quantise_state(r)
+
+        for t in range(-1, ROUNDS + BEHIND):
+            extend(t, CHAIN_C, 1)
+            if t >= 0:
+                quantise_state(t + AHEAD - 1)
+            join_short_chains(t)
+            begin(t + 1, CHAIN_A)
+            extend(t, CHAIN_A, 3)
+            join_all(t)
+            begin(t + 1, CHAIN_B)
+            extend(t + 1, CHAIN_A, 1)
+            begin(t + 1, CHAIN_C)
+            extend(t + 1, CHAIN_B, 1)
+            transpose_result(t - BEHIND)
+            transpose_state(t + AHEAD)
+            store_result(t - BEHIND)
+            regroup_state(t + AHEAD)
+            extend(t + 1, CHAIN_A, 2)

@@ -226,7 +226,7 @@ def tile_ac_filter_prenorm_net_nd_pa_t_kernel(tc, state, Wg, Mg, bg, out):
             regroup_state(r)
             quantise_state(r)
 
-        for t in range(-1, ROUNDS + BEHIND):
+        for t in range(-1, ROUNDS - 2):
             extend(t, CHAIN_C, 1)
             if t >= 0:
                 quantise_state(t + AHEAD - 1)
@@ -243,3 +243,45 @@ def tile_ac_filter_prenorm_net_nd_pa_t_kernel(tc, state, Wg, Mg, bg, out):
             store_result(t - BEHIND)
             regroup_state(t + AHEAD)
             extend(t + 1, CHAIN_A, 2)
+
+        last = ROUNDS - 1
+        extend(last - 1, CHAIN_C, 1)
+        join_short_chains(last - 1)
+        begin(last, CHAIN_B)
+        extend(last - 1, CHAIN_A, 3)
+        join_all(last - 1)
+        begin(last, CHAIN_A)
+        extend(last, CHAIN_B, 1)
+        begin(last, CHAIN_C)
+        extend(last, CHAIN_A, 1)
+        transpose_result(last - 3)
+        transpose_result(last - 2)
+        store_result(last - 3)
+        extend(last, CHAIN_C, 1)
+        join_short_chains(last)
+        store_result(last - 2)
+        extend(last, CHAIN_A, 2)
+        extend(last, CHAIN_A, 3)
+        transpose_result(last - 1)
+        store_result(last - 1)
+        result = stage.tile([P, ROUND], F32, bufs=1, tag="last_result")
+        out_sb = stage.tile([P, ROUND], F32, bufs=1, tag="last_out")
+        for h in range(2):
+            cols = slice(h * ROUND // 2, (h + 1) * ROUND // 2)
+            nc.vector.tensor_tensor(
+                out=result[:, cols],
+                in0=chains[(last, CHAIN_B)][:, cols],
+                in1=chains[(last, CHAIN_A)][:, cols],
+                op=MULT,
+            )
+        for h in range(2):
+            cols = slice(h * ROUND // 2, (h + 1) * ROUND // 2)
+            back = next_bank()
+            for a in range(2):
+                piece = slice((2 * h + a) * P, (2 * h + a + 1) * P)
+                nc.tensor.transpose(back[:, a * P : (a + 1) * P], result[:, piece], identity[:])
+            if h == 0:
+                nc.scalar.copy(out=out_sb[:, cols], in_=back[:, : ROUND // 2])
+            else:
+                nc.vector.tensor_copy(out=out_sb[:, cols], in_=back[:, : ROUND // 2])
+            nc.sync.dma_start(out=out_rounds[last][:, cols], in_=out_sb[:, cols])

@@ -81,15 +81,13 @@ def tile_ac_filter_prenorm_net_nd_pa_t_kernel(tc, state, Wg, Mg, bg, out):
             bank = psum.tile([P, ROUND], F32, tag="bank")
             return bank
 
-        def transpose_pair(words):
+        def transpose_pair(words, split=False):
             flipped = next_bank()
             for b in range(PAIR):
                 for u in range(2):
-                    nc.tensor.transpose(
-                        flipped[:, u * PAIR_ROWS + b * P : u * PAIR_ROWS + (b + 1) * P],
-                        words[:, b * WORDS + u : (b + 1) * WORDS : 2],
-                        identity[:],
-                    )
+                    cols = slice(u * PAIR_ROWS + b * P, u * PAIR_ROWS + (b + 1) * P)
+                    source = words[:, cols] if split else words[:, b * WORDS + u : (b + 1) * WORDS : 2]
+                    nc.tensor.transpose(flipped[:, cols], source, identity[:])
             return flipped
 
         def regroup_pair(flipped, grouped):
@@ -100,6 +98,7 @@ def tile_ac_filter_prenorm_net_nd_pa_t_kernel(tc, state, Wg, Mg, bg, out):
 
         flipped_state = {}
         grouped_state = {}
+        spread_tiles = {}
         quantised = {}
         chains = {}
         results = {}
@@ -108,11 +107,36 @@ def tile_ac_filter_prenorm_net_nd_pa_t_kernel(tc, state, Wg, Mg, bg, out):
         def is_round(r):
             return 0 <= r < ROUNDS
 
+        def spread_blocks_of(r):
+            return 1 if r >= AHEAD else 0
+
+        def spread_state(r):
+            if is_round(r) and spread_blocks_of(r) > 0:
+                n = spread_blocks_of(r)
+                spread = stage.tile([P, ROUND_BLOCKS, E], BF16, tag="spread", bufs=2)
+                for a in range(ROUND_BLOCKS - n, ROUND_BLOCKS):
+                    nc.scalar.copy(
+                        out=spread[:, a].bitcast(F32).rearrange("p (u i) -> p u i", u=2),
+                        in_=state_sb[r][:, a * E : (a + 1) * E].bitcast(F32).rearrange("p (i u) -> p u i", u=2),
+                    )
+                spread_tiles[r] = spread
+
         def transpose_state(r):
             if is_round(r):
                 words = state_sb[r][:].bitcast(F32)
-                half_words = PAIR * WORDS
-                flipped_state[r] = [transpose_pair(words[:, h * half_words : (h + 1) * half_words]) for h in range(2)]
+                flipped_state[r] = []
+                for h in range(2):
+                    flipped = next_bank()
+                    for b in range(PAIR):
+                        a = h * PAIR + b
+                        for u in range(2):
+                            cols = slice(u * PAIR_ROWS + b * P, u * PAIR_ROWS + (b + 1) * P)
+                            if a >= ROUND_BLOCKS - spread_blocks_of(r):
+                                source = spread_tiles[r][:, a].bitcast(F32)[:, u * P : (u + 1) * P]
+                            else:
+                                source = words[:, a * WORDS + u : (a + 1) * WORDS : 2]
+                            nc.tensor.transpose(flipped[:, cols], source, identity[:])
+                    flipped_state[r].append(flipped)
 
         def regroup_state(r):
             if is_round(r):
@@ -198,8 +222,8 @@ def tile_ac_filter_prenorm_net_nd_pa_t_kernel(tc, state, Wg, Mg, bg, out):
 
         w_codes = keep.tile([P, FORMS * P], U32, align_bytes=64)
         w_scales = keep.tile([P, FORMS * P], U8, align_bytes=64)
-        w_grouped = []
-        quantise_lag = 2
+        w_grouped = {}
+        masked_pairs = {}
 
         def quantise_weights(pair):
             cols = slice(pair * PAIR_ROWS, (pair + 1) * PAIR_ROWS)
@@ -207,19 +231,31 @@ def tile_ac_filter_prenorm_net_nd_pa_t_kernel(tc, state, Wg, Mg, bg, out):
                 out=w_codes[:, cols].bitcast(FP8X4), scales=w_scales[:, cols], in_=w_grouped[pair][:]
             )
 
+        def mask_weights(pair):
+            masked = keep.tile([P, PAIR * E], BF16, name="masked_%d" % pair)
+            nc.vector.tensor_tensor(
+                out=masked[:].rearrange("p (u i e) -> p u i e", u=2, e=2),
+                in0=wg_sb[pair][:].rearrange("p (i u e) -> p u i e", u=2, e=2),
+                in1=mg_sb[pair][:].rearrange("p (i u e) -> p u i e", u=2, e=2),
+                op=MULT,
+            )
+            masked_pairs[pair] = masked
+
+        def group_weights(pair):
+            grouped = keep.tile([P, PAIR_ROWS * 4], BF16, align_bytes=64, name="w_grouped_%d" % pair)
+            regroup_pair(transpose_pair(masked_pairs[pair][:].bitcast(F32), True), grouped[:])
+            w_grouped[pair] = grouped
+
         transpose_state(0)
         regroup_state(0)
         for pair in range(WEIGHT_PAIRS):
-            masked = keep.tile([P, PAIR * E], BF16, name="masked_%d" % pair)
-            nc.vector.tensor_tensor(out=masked[:], in0=wg_sb[pair][:], in1=mg_sb[pair][:], op=MULT)
+            mask_weights(pair)
             if pair == 0:
                 quantise_state(0)
-            grouped = keep.tile([P, PAIR_ROWS * 4], BF16, align_bytes=64, name="w_grouped_%d" % pair)
-            regroup_pair(transpose_pair(masked[:].bitcast(F32)), grouped[:])
-            w_grouped.append(grouped)
-            if pair >= quantise_lag:
-                quantise_weights(pair - quantise_lag)
-        for pair in range(WEIGHT_PAIRS - quantise_lag, WEIGHT_PAIRS):
+            group_weights(pair)
+            if pair >= 2:
+                quantise_weights(pair - 2)
+        for pair in range(WEIGHT_PAIRS - 2, WEIGHT_PAIRS):
             quantise_weights(pair)
         for r in range(1, AHEAD - 1):
             transpose_state(r)
@@ -242,6 +278,7 @@ def tile_ac_filter_prenorm_net_nd_pa_t_kernel(tc, state, Wg, Mg, bg, out):
             transpose_state(t + AHEAD)
             store_result(t - BEHIND)
             regroup_state(t + AHEAD)
+            spread_state(t + AHEAD + 1)
             extend(t + 1, CHAIN_A, 2)
 
         last = ROUNDS - 1

@@ -148,8 +148,8 @@ def tile_ac_filter_prenorm_net_nd_pa_t_kernel(tc, state, Wg, Mg, bg, out):
 
         def quantise_state(r):
             if is_round(r):
-                codes = stage.tile([P, ROUND], U32, align_bytes=64, tag="x_codes", bufs=AHEAD + 1)
-                scales = stage.tile([P, ROUND], U8, align_bytes=64, tag="x_scales", bufs=AHEAD + 1)
+                codes = stage.tile([P, ROUND], U32, align_bytes=256, tag="x_codes", bufs=AHEAD + 1)
+                scales = stage.tile([P, ROUND], U8, align_bytes=256, tag="x_scales", bufs=AHEAD + 1)
                 nc.vector.quantize_mx(out=codes[:].bitcast(FP8X4), scales=scales[:], in_=grouped_state[r][:])
                 quantised[r] = (codes, scales)
 
@@ -220,8 +220,8 @@ def tile_ac_filter_prenorm_net_nd_pa_t_kernel(tc, state, Wg, Mg, bg, out):
                 nc.scalar.copy(out=out_sb[:], in_=backs[r][:])
                 nc.sync.dma_start(out=out_rounds[r], in_=out_sb[:])
 
-        w_codes = keep.tile([P, FORMS * P], U32, align_bytes=64)
-        w_scales = keep.tile([P, FORMS * P], U8, align_bytes=64)
+        w_codes = keep.tile([P, FORMS * P], U32, align_bytes=256)
+        w_scales = keep.tile([P, FORMS * P], U8, align_bytes=256)
         w_grouped = {}
         masked_pairs = {}
 

from contextlib import ExitStack

import concourse.mybir as mybir
from concourse.masks import make_identity

FP8X4 = mybir.dt.float8_e4m3fn_x4
BF16 = mybir.dt.bfloat16
F32 = mybir.dt.float32
U32 = mybir.dt.uint32
U8 = mybir.dt.uint8
ADD = mybir.AluOpType.add
MULT = mybir.AluOpType.mult
IDENTITY = mybir.ActivationFunctionType.Identity

P = 128
E = 512
WORDS = E // 2
TOKENS = 8 * 1024
FORMS = 8
ROUND = 512
ROUNDS = TOKENS // ROUND
ROUND_BLOCKS = ROUND // P
PAIR = 2
PAIR_ROWS = PAIR * P
WEIGHT_PAIRS = FORMS // PAIR
BANKS = 8
AHEAD = 3
BEHIND = 2
PARTIALS = 9

CHAIN_A = (0, 1, 2, 3)
CHAIN_B = (4, 5)
CHAIN_C = (6, 7)

FLOPS = 2 * TOKENS * P * FORMS * E


def tile_ac_filter_prenorm_net_nd_pa_t_kernel(tc, state, Wg, Mg, bg, out):
    nc = tc.nc

    state_rounds = state.flatten_outer_dims().rearrange("(r p a) e -> r p (a e)", p=P, a=ROUND_BLOCKS)
    out_rounds = out.flatten_outer_dims().rearrange("(r p a) c -> r p (a c)", p=P, a=ROUND_BLOCKS)
    wg_rows = Wg.rearrange("c j e -> c (j e)")
    mg_rows = Mg.rearrange("c j e -> c (j e)")

    with ExitStack() as ctx:
        keep = ctx.enter_context(tc.tile_pool(name="keep", bufs=1))
        stage = ctx.enter_context(tc.tile_pool(name="stage", bufs=2))
        psum = ctx.enter_context(tc.psum_pool(name="psum", bufs=BANKS))
        ctx.enter_context(tc.manual_schedule())

        bg_sb = keep.tile([P, FORMS], BF16)
        nc.scalar.dma_start(out=bg_sb[:], in_=bg)
        state_sb = []
        wg_sb = []
        mg_sb = []

        def load_state(r):
            state_round = keep.tile([P, ROUND_BLOCKS * E], BF16, name="state_%d" % r)
            nc.sync.dma_start(out=state_round[:], in_=state_rounds[r])
            state_sb.append(state_round)

        load_state(0)
        for pair in range(WEIGHT_PAIRS):
            cols = slice(pair * PAIR * E, (pair + 1) * PAIR * E)
            wg_pair = keep.tile([P, PAIR * E], BF16, name="wg_%d" % pair)
            mg_pair = keep.tile([P, PAIR * E], BF16, name="mg_%d" % pair)
            nc.sync.dma_start(out=wg_pair[:], in_=wg_rows[:, cols])
            nc.sync.dma_start(out=mg_pair[:], in_=mg_rows[:, cols])
            wg_sb.append(wg_pair)
            mg_sb.append(mg_pair)
        for r in range(1, ROUNDS):
            load_state(r)

        identity = keep.tile([P, P], F32)
        make_identity(nc, identity[:])
        bias = keep.tile([P, FORMS], F32)
        nc.scalar.activation(out=bias[:], in_=bg_sb[:], func=IDENTITY)

        def next_bank():
            bank = psum.tile([P, ROUND], F32, tag="bank")
            return bank

        def transpose_pair(words, split=False):
            flipped = next_bank()
            for b in range(PAIR):
                for u in range(2):
                    cols = slice(u * PAIR_ROWS + b * P, u * PAIR_ROWS + (b + 1) * P)
                    source = words[:, cols] if split else words[:, b * WORDS + u : (b + 1) * WORDS : 2]
                    nc.tensor.transpose(flipped[:, cols], source, identity[:])
            return flipped

        def regroup_pair(flipped, grouped):
            nc.scalar.copy(
                out=grouped.bitcast(F32).rearrange("p (n u) -> p n u", u=2),
                in_=flipped[:].rearrange("p (u n) -> p n u", u=2),
            )

        flipped_state = {}
        grouped_state = {}
        spread_tiles = {}
        quantised = {}
        chains = {}
        results = {}
        backs = {}

        def is_round(r):
            return 0 <= r < ROUNDS

        def spread_blocks_of(r):
            return 1 if r >= AHEAD else 0

        def spread_state(r):
            if is_round(r) and spread_blocks_of(r) > 0:
                n = spread_blocks_of(r)
                spread = stage.tile([P, ROUND_BLOCKS, E], BF16, tag="spread", bufs=2)
                for a in range(ROUND_BLOCKS - n, ROUND_BLOCKS):
                    nc.scalar.copy(
                        out=spread[:, a].bitcast(F32).rearrange("p (u i) -> p u i", u=2),
                        in_=state_sb[r][:, a * E : (a + 1) * E].bitcast(F32).rearrange("p (i u) -> p u i", u=2),
                    )
                spread_tiles[r] = spread

        def transpose_state(r):
            if is_round(r):
                words = state_sb[r][:].bitcast(F32)
                flipped_state[r] = []
                for h in range(2):
                    flipped = next_bank()
                    for b in range(PAIR):
                        a = h * PAIR + b
                        for u in range(2):
                            cols = slice(u * PAIR_ROWS + b * P, u * PAIR_ROWS + (b + 1) * P)
                            if a >= ROUND_BLOCKS - spread_blocks_of(r):
                                source = spread_tiles[r][:, a].bitcast(F32)[:, u * P : (u + 1) * P]
                            else:
                                source = words[:, a * WORDS + u : (a + 1) * WORDS : 2]
                            nc.tensor.transpose(flipped[:, cols], source, identity[:])
                    flipped_state[r].append(flipped)

        def regroup_state(r):
            if is_round(r):
                grouped = stage.tile([P, ROUND * 4], BF16, align_bytes=64)
                half_cols = PAIR_ROWS * 4
                for h in range(2):
                    regroup_pair(flipped_state[r][h], grouped[:, h * half_cols : (h + 1) * half_cols])
                grouped_state[r] = grouped

        def quantise_state(r):
            if is_round(r):
                codes = stage.tile([P, ROUND], U32, align_bytes=256, tag="x_codes", bufs=AHEAD + 1)
                scales = stage.tile([P, ROUND], U8, align_bytes=256, tag="x_scales", bufs=AHEAD + 1)
                nc.vector.quantize_mx(out=codes[:].bitcast(FP8X4), scales=scales[:], in_=grouped_state[r][:])
                quantised[r] = (codes, scales)

        def form(r, j):
            bank = next_bank()
            codes, scales = quantised[r]
            cols = slice(j * P, (j + 1) * P)
            nc.tensor.matmul_mx(
                out=bank[:],
                lhsT=w_codes[:, cols].bitcast(FP8X4),
                lhsT_scale=w_scales[:, cols],
                rhs=codes[:].bitcast(FP8X4),
                rhs_scale=scales[:],
                start=True,
                stop=True,
            )
            return bank

        def partial():
            product = stage.tile([P, ROUND], F32, tag="partial", bufs=3 * PARTIALS)
            return product

        def begin(r, chain):
            if is_round(r):
                j = chain[0]
                bank = form(r, j)
                chains[(r, chain)] = partial()
                nc.scalar.activation(
                    out=chains[(r, chain)][:], in_=bank[:], func=IDENTITY, bias=bias[:, j : j + 1], scale=1.0
                )

        def extend(r, chain, i):
            if is_round(r):
                j = chain[i]
                bank = form(r, j)
                longer = partial()
                nc.vector.scalar_tensor_tensor(
                    out=longer[:], in0=bank[:], scalar=bias[:, j : j + 1], in1=chains[(r, chain)][:], op0=ADD, op1=MULT
                )
                chains[(r, chain)] = longer

        def join_short_chains(r):
            if is_round(r):
                joined = partial()
                nc.gpsimd.tensor_tensor(
                    out=joined[:], in0=chains[(r, CHAIN_B)][:], in1=chains[(r, CHAIN_C)][:], op=MULT
                )
                chains[(r, CHAIN_B)] = joined

        def join_all(r):
            if is_round(r):
                result = stage.tile([P, ROUND], F32, bufs=BEHIND + 2)
                nc.gpsimd.tensor_tensor(
                    out=result[:], in0=chains[(r, CHAIN_B)][:], in1=chains[(r, CHAIN_A)][:], op=MULT
                )
                results[r] = result

        def transpose_result(r):
            if is_round(r):
                backs[r] = next_bank()
                for a in range(ROUND_BLOCKS):
                    cols = slice(a * P, (a + 1) * P)
                    nc.tensor.transpose(backs[r][:, cols], results[r][:, cols], identity[:])

        def store_result(r):
            if is_round(r):
                out_sb = stage.tile([P, ROUND], F32, bufs=3)
                nc.scalar.copy(out=out_sb[:], in_=backs[r][:])
                nc.sync.dma_start(out=out_rounds[r], in_=out_sb[:])

        w_codes = keep.tile([P, FORMS * P], U32, align_bytes=256)
        w_scales = keep.tile([P, FORMS * P], U8, align_bytes=256)
        w_grouped = {}
        masked_pairs = {}

        def quantise_weights(pair):
            cols = slice(pair * PAIR_ROWS, (pair + 1) * PAIR_ROWS)
            nc.vector.quantize_mx(
                out=w_codes[:, cols].bitcast(FP8X4), scales=w_scales[:, cols], in_=w_grouped[pair][:]
            )

        def mask_weights(pair):
            masked = keep.tile([P, PAIR * E], BF16, name="masked_%d" % pair)
            nc.vector.tensor_tensor(
                out=masked[:].rearrange("p (u i e) -> p u i e", u=2, e=2),
                in0=wg_sb[pair][:].rearrange("p (i u e) -> p u i e", u=2, e=2),
                in1=mg_sb[pair][:].rearrange("p (i u e) -> p u i e", u=2, e=2),
                op=MULT,
            )
            masked_pairs[pair] = masked

        def group_weights(pair):
            grouped = keep.tile([P, PAIR_ROWS * 4], BF16, align_bytes=64, name="w_grouped_%d" % pair)
            regroup_pair(transpose_pair(masked_pairs[pair][:].bitcast(F32), True), grouped[:])
            w_grouped[pair] = grouped

        transpose_state(0)
        regroup_state(0)
        for pair in range(WEIGHT_PAIRS):
            mask_weights(pair)
            if pair == 0:
                quantise_state(0)
            group_weights(pair)
            if pair >= 2:
                quantise_weights(pair - 2)
        for pair in range(WEIGHT_PAIRS - 2, WEIGHT_PAIRS):
            quantise_weights(pair)
        for r in range(1, AHEAD - 1):
            transpose_state(r)
            regroup_state(r)
            quantise_state(r)

        for t in range(-1, ROUNDS - 2):
            extend(t, CHAIN_C, 1)
            if t >= 0:
                quantise_state(t + AHEAD - 1)
            join_short_chains(t)
            begin(t + 1, CHAIN_A)
            extend(t, CHAIN_A, 3)
            join_all(t)
            begin(t + 1, CHAIN_B)
            extend(t + 1, CHAIN_A, 1)
            begin(t + 1, CHAIN_C)
            extend(t + 1, CHAIN_B, 1)
            transpose_result(t - BEHIND)
            transpose_state(t + AHEAD)
            store_result(t - BEHIND)
            regroup_state(t + AHEAD)
            spread_state(t + AHEAD + 1)
            extend(t + 1, CHAIN_A, 2)

        last = ROUNDS - 1
        extend(last - 1, CHAIN_C, 1)
        join_short_chains(last - 1)
        begin(last, CHAIN_B)
        extend(last - 1, CHAIN_A, 3)
        join_all(last - 1)
        begin(last, CHAIN_A)
        extend(last, CHAIN_B, 1)
        begin(last, CHAIN_C)
        extend(last, CHAIN_A, 1)
        transpose_result(last - 3)
        transpose_result(last - 2)
        store_result(last - 3)
        extend(last, CHAIN_C, 1)
        join_short_chains(last)
        store_result(last - 2)
        extend(last, CHAIN_A, 2)
        extend(last, CHAIN_A, 3)
        transpose_result(last - 1)
        store_result(last - 1)
        result = stage.tile([P, ROUND], F32, bufs=1, tag="last_result")
        out_sb = stage.tile([P, ROUND], F32, bufs=1, tag="last_out")
        for h in range(2):
            cols = slice(h * ROUND // 2, (h + 1) * ROUND // 2)
            nc.vector.tensor_tensor(
                out=result[:, cols],
                in0=chains[(last, CHAIN_B)][:, cols],
                in1=chains[(last, CHAIN_A)][:, cols],
                op=MULT,
            )
        for h in range(2):
            cols = slice(h * ROUND // 2, (h + 1) * ROUND // 2)
            back = next_bank()
            for a in range(2):
                piece = slice((2 * h + a) * P, (2 * h + a + 1) * P)
                nc.tensor.transpose(back[:, a * P : (a + 1) * P], result[:, piece], identity[:])
            if h == 0:
                nc.scalar.copy(out=out_sb[:, cols], in_=back[:, : ROUND // 2])
            else:
                nc.vector.tensor_copy(out=out_sb[:, cols], in_=back[:, : ROUND // 2])
            nc.sync.dma_start(out=out_rounds[last][:, cols], in_=out_sb[:, cols])
